import numpy as np
import ml_dtypes


def mxq(x, axis, fmt="e4m3"):
    dtype, down = {"e4m3": (ml_dtypes.float8_e4m3fn, 7), "e5m2": (ml_dtypes.float8_e5m2, 14)}[fmt]
    v = np.moveaxis(np.asarray(x, np.float32).astype(ml_dtypes.bfloat16).astype(np.float64), axis, -1)
    blocks = v.reshape(v.shape[:-1] + (-1, 32))
    amax = np.abs(blocks).max(-1, keepdims=True)
    byte = np.maximum(np.where(amax > 0, np.frexp(amax)[1] - 1 + 127, 0) - down, 1)
    scale = np.exp2(byte - 127.0)
    codes = (blocks / scale).astype(np.float32).astype(dtype).astype(np.float64)
    return np.moveaxis((codes * scale).reshape(v.shape), -1, axis)


WIDE = False


def mx_kscale(k):
    if not WIDE:
        return np.ones(k)
    levels = np.array([10, -10, 5, -5, 0])
    if k % 512:
        return np.exp2(np.random.permutation(np.resize(levels, k // 32))).repeat(32)
    a = np.empty((k // 512, 16))
    for p in range(k // 512):
        a[p, :8] = np.random.permutation(np.resize(levels, 8))
        for g in range(8):
            far = levels[np.abs(levels - a[p, g]) >= 10]
            a[p, g + 8] = far[np.random.randint(len(far))]
    return np.exp2(a.ravel()).repeat(32)


BF16 = ml_dtypes.bfloat16


def bf(x):
    return np.asarray(x, np.float32).astype(BF16)


def f64(x):
    return np.asarray(x).astype(np.float64)


B, D0, D1, D2, D3 = 512, 2048, 2048, 2048, 2048
HEBB = 0.01
RATE = 0.001
BATCH_NUM = 1
C = HEBB * RATE / BATCH_NUM


def centred(s):
    return s / np.exp2(np.round(np.log2(s.mean())))


def setup_inputs():
    s = centred(mx_kscale(D2))
    return {"vi": bf(np.maximum(3.0 + 5.0 * np.random.standard_normal((B, D2)), 0.0) * s),
            "W": bf(np.random.standard_normal((D3, D2)) * 0.9 / np.sqrt(D2) / s[None, :]),
            "b": bf(3.0 + 1.5 * np.random.standard_normal(D3))}


def reference(vi, W, b):
    vi = f64(vi)
    vj = np.maximum((mxq(vi, 1, "e4m3") @ mxq(f64(W), 1, "e4m3").T) + f64(b), 0.0)
    m = np.mean(vj, axis=0)
    out = vj + np.sum(vi, axis=1, keepdims=True) * (C * m)[None, :]
    return out, m

@@ -1,0 +1,263 @@
+from contextlib import ExitStack
+
+import concourse.mybir as mybir
+from concourse.masks import make_identity
+
+F32 = mybir.dt.float32
+BF16 = mybir.dt.bfloat16
+U32 = mybir.dt.uint32
+U8 = mybir.dt.uint8
+FP8X4 = mybir.dt.float8_e4m3fn_x4
+ALU = mybir.AluOpType
+ACT = mybir.ActivationFunctionType
+AXIS = mybir.AxisListType
+
+P = 128
+PACK = 4
+K_PASS = P * PACK
+ROWS = 512
+K = 2048
+OUTS = 2048
+PASSES = K // K_PASS
+ROW_TILES = ROWS // P
+OUT_TILES = OUTS // P
+HALVES = 2
+PASSES_PER_BANK = PASSES // HALVES
+K_HALF = K // HALVES
+WORDS_PER_PASS = K_PASS // 2
+TILE_COLS = PASSES * P * PACK
+
+STEP = 2
+STEPS = OUT_TILES // STEP
+BACK_LAG = 2
+PRODUCT_BANKS = STEP
+TRANSPOSE_BANKS = 8 - PRODUCT_BANKS
+
+C = 0.01 * 0.001 / 1
+FLOPS = 2 * ROWS * K * OUTS
+
+
+def transpose_words(nc, bank, words, ident):
+    for i in range(PASSES_PER_BANK):
+        for u in range(2):
+            every_second = slice(i * WORDS_PER_PASS + u, (i + 1) * WORDS_PER_PASS, 2)
+            nc.tensor.transpose(bank[:, i, u, :], words[:, every_second], ident[:])
+
+
+def empty_bank(nc, by_vector, out, in_):
+    if by_vector:
+        nc.vector.tensor_copy(out=out, in_=in_)
+    else:
+        nc.scalar.copy(out=out, in_=in_)
+
+
+def tile_optimalnet_pb_kernel(tc, vi, W, b, out_0, out_1):
+    nc = tc.nc
+    with ExitStack() as stack:
+        keep = stack.enter_context(tc.tile_pool(name="keep", bufs=1))
+        weights = stack.enter_context(tc.tile_pool(name="weights", bufs=STEPS))
+        work = stack.enter_context(tc.tile_pool(name="work", bufs=2 * STEP))
+        psum = stack.enter_context(tc.psum_pool(name="psum", bufs=PRODUCT_BANKS))
+
+        b_rows = keep.tile([OUT_TILES, P], BF16)
+        nc.scalar.dma_start(out=b_rows[:], in_=b.rearrange("(j p) -> j p", p=P))
+        vi_rows = {}
+        for rt in range(ROW_TILES):
+            for half in range(HALVES):
+                rows = keep.tile([P, K_HALF], BF16, name="vi_rows%d_%d" % (rt, half))
+                nc.sync.dma_start(
+                    out=rows[:], in_=vi[rt * P : (rt + 1) * P, half * K_HALF : (half + 1) * K_HALF]
+                )
+                vi_rows[rt, half] = rows
+        w_rows = []
+        for s in range(STEPS):
+            rows = weights.tile([P, STEP, K], BF16, name="w_rows")
+            first = s * STEP * P
+            nc.sync.dma_start(
+                out=rows[:], in_=W[first : first + STEP * P, :].rearrange("(a p) k -> p a k", p=P)
+            )
+            w_rows.append(rows)
+
+        ident = keep.tile([P, P], F32)
+        make_identity(nc, ident[:])
+        ones = keep.tile([P, P], BF16)
+        nc.vector.memset(ones[:], 1.0)
+        b_square = keep.tile([P, P], F32)
+        nc.vector.memset(b_square[:], 0.0)
+        colsum = keep.tile([P, P], F32)
+        nc.vector.memset(colsum[:], 0.0)
+        nc.vector.tensor_copy(out=b_square[0:OUT_TILES, :], in_=b_rows[:])
+        b_col = keep.tile([P, OUT_TILES], F32)
+
+        vi_grouped = keep.tile([P, PASSES * ROWS * PACK], BF16, align_bytes=64)
+        vi_grouped_words = vi_grouped[:].bitcast(F32).rearrange("p (g r u) -> p g r u", g=PASSES, u=2)
+        vi_grouped_cols = vi_grouped[:].rearrange("p (g c) -> p g c", g=PASSES)
+        vi_codes = keep.tile([P, PASSES, ROWS], U32, align_bytes=64)
+        vi_scales = keep.tile([P, PASSES, ROWS], U8, align_bytes=64)
+        rowsum_raw = keep.tile([P, ROWS], F32)
+        rowsum_scaled = keep.tile([P, ROWS], F32)
+
+        def vi_transpose_and_regroup(rt):
+            for half in range(HALVES):
+                bank = psum.tile([P, PASSES_PER_BANK, 2, P], F32, tag="transposed", bufs=TRANSPOSE_BANKS)
+                transpose_words(nc, bank, vi_rows[rt, half][:].bitcast(F32), ident)
+                nc.scalar.copy(
+                    out=vi_grouped_words[
+                        :, half * PASSES_PER_BANK : (half + 1) * PASSES_PER_BANK, rt * P : (rt + 1) * P, :
+                    ],
+                    in_=bank[:].rearrange("p i u r -> p i r u"),
+                )
+
+        def vi_quantise(rt):
+            for g in range(PASSES):
+                nc.vector.quantize_mx(
+                    out=vi_codes[:, g, rt * P : (rt + 1) * P].bitcast(FP8X4),
+                    scales=vi_scales[:, g, rt * P : (rt + 1) * P],
+                    in_=vi_grouped_cols[:, g, rt * P * PACK : (rt + 1) * P * PACK],
+                )
+
+        def vi_sum_rows(rt):
+            partial = psum.tile([P, P * PACK], F32, tag="product")
+            for g in range(PASSES):
+                nc.tensor.matmul(
+                    out=partial[:],
+                    lhsT=ones[:],
+                    rhs=vi_grouped_cols[:, g, rt * P * PACK : (rt + 1) * P * PACK],
+                    start=(g == 0),
+                    stop=(g == PASSES - 1),
+                )
+            nc.vector.tensor_reduce(
+                out=rowsum_raw[:, rt * P : (rt + 1) * P],
+                in_=partial[:].rearrange("p (r t) -> p r t", t=PACK),
+                axis=AXIS.X,
+                op=ALU.add,
+            )
+
+        w_banks = {}
+        w_grouped = {}
+        w_codes = {}
+        w_scales = {}
+        product = {}
+        vj = {}
+        back = {}
+
+        def tiles_of(s):
+            return range(s * STEP, (s + 1) * STEP)
+
+        def w_transpose(s):
+            for j in tiles_of(s):
+                for half in range(HALVES):
+                    bank = psum.tile([P, PASSES_PER_BANK, 2, P], F32, tag="transposed", bufs=TRANSPOSE_BANKS)
+                    half_rows = w_rows[s][:, j - s * STEP, half * K_HALF : (half + 1) * K_HALF]
+                    transpose_words(nc, bank, half_rows.bitcast(F32), ident)
+                    w_banks[j, half] = bank
+
+        def w_regroup(s):
+            for j in tiles_of(s):
+                w_grouped[j] = work.tile([P, TILE_COLS], BF16, name="w_grouped", align_bytes=64)
+                grouped_words = w_grouped[j][:].bitcast(F32).rearrange("p (g o u) -> p g o u", g=PASSES, u=2)
+                for half in range(HALVES):
+                    empty_bank(
+                        nc,
+                        by_vector=(j == s * STEP and half == 0),
+                        out=grouped_words[:, half * PASSES_PER_BANK : (half + 1) * PASSES_PER_BANK],
+                        in_=w_banks[j, half][:].rearrange("p i u o -> p i o u"),
+                    )
+
+        def w_quantise(s):
+            for j in tiles_of(s):
+                w_codes[j] = work.tile([P, PASSES * P], U32, name="w_codes", align_bytes=64)
+                w_scales[j] = work.tile([P, PASSES * P], U8, name="w_scales", align_bytes=64)
+                nc.vector.quantize_mx(
+                    out=w_codes[j][:].bitcast(FP8X4), scales=w_scales[j][:], in_=w_grouped[j][:]
+                )
+
+        def multiply(s):
+            for j in tiles_of(s):
+                product[j] = psum.tile([P, ROWS], F32, name="product", tag="product")
+                for g in range(PASSES):
+                    nc.tensor.matmul_mx(
+                        out=product[j][:],
+                        lhsT=w_codes[j][:, g * P : (g + 1) * P].bitcast(FP8X4),
+                        lhsT_scale=w_scales[j][:, g * P : (g + 1) * P],
+                        rhs=vi_codes[:, g, :].bitcast(FP8X4),
+                        rhs_scale=vi_scales[:, g, :],
+                        start=(g == 0),
+                        stop=(g == PASSES - 1),
+                    )
+
+        def bias_relu_and_sum(s):
+            for j in tiles_of(s):
+                vj[j] = work.tile([P, ROWS], F32, name="vj", bufs=(BACK_LAG + 1) * STEP)
+                nc.scalar.activation(
+                    out=vj[j][:],
+                    in_=product[j][:],
+                    func=ACT.Relu,
+                    bias=b_col[:, j : j + 1],
+                    scale=1.0,
+                    accum_out=colsum[:, j : j + 1],
+                )
+
+        def correct(s):
+            for j in tiles_of(s):
+                nc.vector.scalar_tensor_tensor(
+                    out=vj[j][:],
+                    in0=rowsum_scaled[:],
+                    scalar=colsum[:, j : j + 1],
+                    in1=vj[j][:],
+                    op0=ALU.mult,
+                    op1=ALU.add,
+                )
+
+        def transpose_back(s):
+            for j in tiles_of(s):
+                back[j] = psum.tile([P, ROW_TILES, P], F32, name="back", tag="transposed", bufs=TRANSPOSE_BANKS)
+                for rt in range(ROW_TILES):
+                    nc.tensor.transpose(back[j][:, rt, :], vj[j][:, rt * P : (rt + 1) * P], ident[:])
+
+        def copy_out_and_store(s):
+            for j in tiles_of(s):
+                result = work.tile([P, ROW_TILES, P], F32, name="result")
+                empty_bank(nc, by_vector=(j == (s + 1) * STEP - 1), out=result[:], in_=back[j][:])
+                nc.sync.dma_start(
+                    out=out_0[:, j * P : (j + 1) * P].rearrange("(t p) o -> p t o", p=P), in_=result[:]
+                )
+
+        def store_mean():
+            sums_as_rows = psum.tile([P, P], F32, tag="transposed", bufs=TRANSPOSE_BANKS)
+            nc.tensor.transpose(sums_as_rows[:], colsum[:], ident[:])
+            mean_rows = keep.tile([OUT_TILES, P], F32)
+            nc.scalar.mul(out=mean_rows[:], in_=sums_as_rows[0:OUT_TILES, :], mul=1.0 / ROWS)
+            nc.sync.dma_start(out=out_1.rearrange("(j p) -> j p", p=P), in_=mean_rows[:])
+
+        for rt in range(ROW_TILES):
+            vi_transpose_and_regroup(rt)
+            if rt == 0:
+                b_as_columns = psum.tile([P, P], F32, tag="transposed", bufs=TRANSPOSE_BANKS)
+                nc.tensor.transpose(b_as_columns[:], b_square[:], ident[:])
+                nc.vector.tensor_copy(out=b_col[:], in_=b_as_columns[:, 0:OUT_TILES])
+            else:
+                vi_sum_rows(rt - 1)
+            vi_quantise(rt)
+        w_transpose(0)
+        w_regroup(0)
+        vi_sum_rows(ROW_TILES - 1)
+        nc.vector.tensor_scalar_mul(out=rowsum_scaled[:], in0=rowsum_raw[:], scalar1=C / ROWS)
+        w_quantise(0)
+
+        for i in range(STEPS + BACK_LAG):
+            if i + 1 < STEPS:
+                w_transpose(i + 1)
+                w_regroup(i + 1)
+            if 1 <= i <= STEPS:
+                correct(i - 1)
+            if i >= BACK_LAG:
+                transpose_back(i - BACK_LAG)
+                copy_out_and_store(i - BACK_LAG)
+            if i == STEPS:
+                store_mean()
+            if i + 1 < STEPS:
+                w_quantise(i + 1)
+            if i < STEPS:
+                multiply(i)
+                bias_relu_and_sum(i)

@@ -37,6 +37,12 @@ C = 0.01 * 0.001 / 1
 FLOPS = 2 * ROWS * K * OUTS
 
 
+def transpose_permuted_words(nc, bank, words, ident):
+    for i in range(PASSES_PER_BANK):
+        for u in range(2):
+            nc.tensor.transpose(bank[:, i, u, :], words[:, i, u, :], ident[:])
+
+
 def transpose_words(nc, bank, words, ident):
     for i in range(PASSES_PER_BANK):
         for u in range(2):
@@ -133,6 +139,7 @@ def tile_optimalnet_pb_kernel(tc, vi, W, b, out_0, out_1):
                 op=ALU.add,
             )
 
+        w_split = {}
         w_banks = {}
         w_grouped = {}
         w_codes = {}
@@ -144,12 +151,20 @@ def tile_optimalnet_pb_kernel(tc, vi, W, b, out_0, out_1):
         def tiles_of(s):
             return range(s * STEP, (s + 1) * STEP)
 
+        def w_split_words(s):
+            for j in tiles_of(s):
+                w_split[j] = work.tile([P, PASSES, 2, P], F32, name="w_split")
+                words = w_rows[s][:, j - s * STEP, :].bitcast(F32)
+                nc.vector.tensor_copy(
+                    out=w_split[j][:], in_=words.rearrange("p (g w u) -> p g u w", g=PASSES, u=2)
+                )
+
         def w_transpose(s):
             for j in tiles_of(s):
                 for half in range(HALVES):
                     bank = psum.tile([P, PASSES_PER_BANK, 2, P], F32, tag="transposed", bufs=TRANSPOSE_BANKS)
-                    half_rows = w_rows[s][:, j - s * STEP, half * K_HALF : (half + 1) * K_HALF]
-                    transpose_words(nc, bank, half_rows.bitcast(F32), ident)
+                    half_words = w_split[j][:, half * PASSES_PER_BANK : (half + 1) * PASSES_PER_BANK]
+                    transpose_permuted_words(nc, bank, half_words, ident)
                     w_banks[j, half] = bank
 
         def w_regroup(s):
@@ -159,7 +174,7 @@ def tile_optimalnet_pb_kernel(tc, vi, W, b, out_0, out_1):
                 for half in range(HALVES):
                     empty_bank(
                         nc,
-                        by_vector=(j == s * STEP and half == 0),
+                        by_vector=False,
                         out=grouped_words[:, half * PASSES_PER_BANK : (half + 1) * PASSES_PER_BANK],
                         in_=w_banks[j, half][:].rearrange("p i u o -> p i o u"),
                     )
@@ -239,13 +254,17 @@ def tile_optimalnet_pb_kernel(tc, vi, W, b, out_0, out_1):
             else:
                 vi_sum_rows(rt - 1)
             vi_quantise(rt)
+        w_split_words(0)
         w_transpose(0)
         w_regroup(0)
+        w_split_words(1)
         vi_sum_rows(ROW_TILES - 1)
         nc.vector.tensor_scalar_mul(out=rowsum_scaled[:], in0=rowsum_raw[:], scalar1=C / ROWS)
         w_quantise(0)
 
         for i in range(STEPS + BACK_LAG):
+            if i + 2 < STEPS:
+                w_split_words(i + 2)
             if i + 1 < STEPS:
                 w_transpose(i + 1)
                 w_regroup(i + 1)

@@ -10,7 +10,6 @@ U8 = mybir.dt.uint8
 FP8X4 = mybir.dt.float8_e4m3fn_x4
 ALU = mybir.AluOpType
 ACT = mybir.ActivationFunctionType
-AXIS = mybir.AxisListType
 
 P = 128
 PACK = 4
@@ -29,93 +28,98 @@ TILE_COLS = PASSES * P * PACK
 
 STEP = 2
 STEPS = OUT_TILES // STEP
-BACK_LAG = 2
-PRODUCT_BANKS = STEP
-TRANSPOSE_BANKS = 8 - PRODUCT_BANKS
+STEP_OUTS = STEP * P
+RT_PER_BANK = 2
+TRANSPOSE_BANKS = 6
+WARM_UPS = 4
 
 C = 0.01 * 0.001 / 1
 FLOPS = 2 * ROWS * K * OUTS
 
 
-def transpose_permuted_words(nc, bank, words, ident):
-    for i in range(PASSES_PER_BANK):
-        for u in range(2):
-            nc.tensor.transpose(bank[:, i, u, :], words[:, i, u, :], ident[:])
-
-
-def transpose_words(nc, bank, words, ident):
+def transpose_every_second_word(nc, bank, words, ident):
     for i in range(PASSES_PER_BANK):
         for u in range(2):
             every_second = slice(i * WORDS_PER_PASS + u, (i + 1) * WORDS_PER_PASS, 2)
             nc.tensor.transpose(bank[:, i, u, :], words[:, every_second], ident[:])
 
 
-def empty_bank(nc, by_vector, out, in_):
-    if by_vector:
-        nc.vector.tensor_copy(out=out, in_=in_)
-    else:
-        nc.scalar.copy(out=out, in_=in_)
+def transpose_split_words(nc, bank, words, ident):
+    for i in range(PASSES_PER_BANK):
+        for u in range(2):
+            nc.tensor.transpose(bank[:, i, u, :], words[:, i, u, :], ident[:])
 
 
 def tile_optimalnet_pb_kernel(tc, vi, W, b, out_0, out_1):
     nc = tc.nc
     with ExitStack() as stack:
         keep = stack.enter_context(tc.tile_pool(name="keep", bufs=1))
-        weights = stack.enter_context(tc.tile_pool(name="weights", bufs=STEPS))
         work = stack.enter_context(tc.tile_pool(name="work", bufs=2 * STEP))
-        psum = stack.enter_context(tc.psum_pool(name="psum", bufs=PRODUCT_BANKS))
+        psum = stack.enter_context(tc.psum_pool(name="psum", bufs=2))
+        stack.enter_context(tc.manual_schedule())
 
         b_rows = keep.tile([OUT_TILES, P], BF16)
         nc.scalar.dma_start(out=b_rows[:], in_=b.rearrange("(j p) -> j p", p=P))
         vi_rows = {}
-        for rt in range(ROW_TILES):
+        w_rows = {}
+
+        def load_vi(rt):
             for half in range(HALVES):
                 rows = keep.tile([P, K_HALF], BF16, name="vi_rows%d_%d" % (rt, half))
                 nc.sync.dma_start(
                     out=rows[:], in_=vi[rt * P : (rt + 1) * P, half * K_HALF : (half + 1) * K_HALF]
                 )
                 vi_rows[rt, half] = rows
-        w_rows = []
-        for s in range(STEPS):
-            rows = weights.tile([P, STEP, K], BF16, name="w_rows")
-            first = s * STEP * P
-            nc.sync.dma_start(
-                out=rows[:], in_=W[first : first + STEP * P, :].rearrange("(a p) k -> p a k", p=P)
-            )
-            w_rows.append(rows)
 
-        ident = keep.tile([P, P], F32)
-        make_identity(nc, ident[:])
-        ones = keep.tile([P, P], BF16)
+        def load_w(j):
+            rows = keep.tile([P, K], BF16, name="w_rows%d" % j)
+            nc.sync.dma_start(out=rows[:], in_=W[j * P : (j + 1) * P, :])
+            w_rows[j] = rows
+
+        for rt in range(ROW_TILES - 1):
+            load_vi(rt)
+        load_w(0)
+        load_vi(ROW_TILES - 1)
+        for j in range(1, OUT_TILES):
+            load_w(j)
+
+        ones = keep.tile([P, ROWS], BF16)
         nc.vector.memset(ones[:], 1.0)
         b_square = keep.tile([P, P], F32)
         nc.vector.memset(b_square[:], 0.0)
-        colsum = keep.tile([P, P], F32)
-        nc.vector.memset(colsum[:], 0.0)
-        nc.vector.tensor_copy(out=b_square[0:OUT_TILES, :], in_=b_rows[:])
+        ident = keep.tile([P, P], F32)
+        make_identity(nc, ident[:])
         b_col = keep.tile([P, OUT_TILES], F32)
+        colsum = keep.tile([P, OUT_TILES], F32)
+        mean = keep.tile([P, OUTS], F32)
+        rowsum = keep.tile([P, ROW_TILES], F32)
+        rowsum_c = keep.tile([P, ROW_TILES], F32)
 
         vi_grouped = keep.tile([P, PASSES * ROWS * PACK], BF16, align_bytes=64)
         vi_grouped_words = vi_grouped[:].bitcast(F32).rearrange("p (g r u) -> p g r u", g=PASSES, u=2)
         vi_grouped_cols = vi_grouped[:].rearrange("p (g c) -> p g c", g=PASSES)
         vi_codes = keep.tile([P, PASSES, ROWS], U32, align_bytes=64)
         vi_scales = keep.tile([P, PASSES, ROWS], U8, align_bytes=64)
-        rowsum_raw = keep.tile([P, ROWS], F32)
-        rowsum_scaled = keep.tile([P, ROWS], F32)
 
-        def vi_transpose_and_regroup(rt):
-            for half in range(HALVES):
-                bank = psum.tile([P, PASSES_PER_BANK, 2, P], F32, tag="transposed", bufs=TRANSPOSE_BANKS)
-                transpose_words(nc, bank, vi_rows[rt, half][:].bitcast(F32), ident)
-                nc.scalar.copy(
-                    out=vi_grouped_words[
-                        :, half * PASSES_PER_BANK : (half + 1) * PASSES_PER_BANK, rt * P : (rt + 1) * P, :
-                    ],
-                    in_=bank[:].rearrange("p i u r -> p i r u"),
-                )
+        def forward_bank():
+            return psum.tile([P, PASSES_PER_BANK, 2, P], F32, name="bank", tag="transposed", bufs=TRANSPOSE_BANKS)
 
-        def vi_quantise(rt):
-            for g in range(PASSES):
+        vi_banks = {}
+
+        def vi_transpose(rt, half):
+            vi_banks[rt, half] = forward_bank()
+            transpose_every_second_word(nc, vi_banks[rt, half], vi_rows[rt, half][:].bitcast(F32), ident)
+
+        def vi_regroup(rt, half):
+            nc.scalar.copy(
+                out=vi_grouped_words[
+                    :, half * PASSES_PER_BANK : (half + 1) * PASSES_PER_BANK, rt * P : (rt + 1) * P, :
+                ],
+                in_=vi_banks[rt, half][:].rearrange("p i u r -> p i r u"),
+            )
+
+        def vi_quantise(rt, half):
+            for g in range(half * PASSES_PER_BANK, (half + 1) * PASSES_PER_BANK):
                 nc.vector.quantize_mx(
                     out=vi_codes[:, g, rt * P : (rt + 1) * P].bitcast(FP8X4),
                     scales=vi_scales[:, g, rt * P : (rt + 1) * P],
@@ -123,20 +127,15 @@ def tile_optimalnet_pb_kernel(tc, vi, W, b, out_0, out_1):
                 )
 
         def vi_sum_rows(rt):
-            partial = psum.tile([P, P * PACK], F32, tag="product")
-            for g in range(PASSES):
-                nc.tensor.matmul(
-                    out=partial[:],
-                    lhsT=ones[:],
-                    rhs=vi_grouped_cols[:, g, rt * P * PACK : (rt + 1) * P * PACK],
-                    start=(g == 0),
-                    stop=(g == PASSES - 1),
-                )
-            nc.vector.tensor_reduce(
-                out=rowsum_raw[:, rt * P : (rt + 1) * P],
-                in_=partial[:].rearrange("p (r t) -> p r t", t=PACK),
-                axis=AXIS.X,
-                op=ALU.add,
+            half_sums = work.tile([P, K_HALF], F32, name="half_sums", bufs=1)
+            nc.vector.scalar_tensor_tensor(
+                out=half_sums[:],
+                in0=vi_rows[rt, 0][:],
+                scalar=1.0,
+                in1=vi_rows[rt, 1][:],
+                op0=ALU.mult,
+                op1=ALU.add,
+                accum_out=rowsum[:, rt : rt + 1],
             )
 
         w_split = {}
@@ -146,137 +145,199 @@ def tile_optimalnet_pb_kernel(tc, vi, W, b, out_0, out_1):
         w_scales = {}
         product = {}
         vj = {}
+        mean_bank = {}
         back = {}
 
-        def tiles_of(s):
-            return range(s * STEP, (s + 1) * STEP)
+        def w_split_words(j):
+            w_split[j] = work.tile([P, PASSES, 2, P], F32, name="w_split")
+            nc.vector.tensor_copy(
+                out=w_split[j][:],
+                in_=w_rows[j][:].bitcast(F32).rearrange("p (g w u) -> p g u w", g=PASSES, u=2),
+            )
 
-        def w_split_words(s):
-            for j in tiles_of(s):
-                w_split[j] = work.tile([P, PASSES, 2, P], F32, name="w_split")
-                words = w_rows[s][:, j - s * STEP, :].bitcast(F32)
-                nc.vector.tensor_copy(
-                    out=w_split[j][:], in_=words.rearrange("p (g w u) -> p g u w", g=PASSES, u=2)
-                )
-
-        def w_transpose(s):
-            for j in tiles_of(s):
-                for half in range(HALVES):
-                    bank = psum.tile([P, PASSES_PER_BANK, 2, P], F32, tag="transposed", bufs=TRANSPOSE_BANKS)
+        def w_transpose(j):
+            for half in range(HALVES):
+                w_banks[j, half] = forward_bank()
+                if j in w_split:
                     half_words = w_split[j][:, half * PASSES_PER_BANK : (half + 1) * PASSES_PER_BANK]
-                    transpose_permuted_words(nc, bank, half_words, ident)
-                    w_banks[j, half] = bank
+                    transpose_split_words(nc, w_banks[j, half], half_words, ident)
+                else:
+                    half_rows = w_rows[j][:, half * K_HALF : (half + 1) * K_HALF]
+                    transpose_every_second_word(nc, w_banks[j, half], half_rows.bitcast(F32), ident)
 
-        def w_regroup(s):
-            for j in tiles_of(s):
+        def w_regroup(j, half, by_vector=False):
+            if half == 0:
                 w_grouped[j] = work.tile([P, TILE_COLS], BF16, name="w_grouped", align_bytes=64)
-                grouped_words = w_grouped[j][:].bitcast(F32).rearrange("p (g o u) -> p g o u", g=PASSES, u=2)
-                for half in range(HALVES):
-                    empty_bank(
-                        nc,
-                        by_vector=False,
-                        out=grouped_words[:, half * PASSES_PER_BANK : (half + 1) * PASSES_PER_BANK],
-                        in_=w_banks[j, half][:].rearrange("p i u o -> p i o u"),
-                    )
+            grouped_words = w_grouped[j][:].bitcast(F32).rearrange("p (g o u) -> p g o u", g=PASSES, u=2)
+            out = grouped_words[:, half * PASSES_PER_BANK : (half + 1) * PASSES_PER_BANK]
+            in_words = w_banks[j, half][:].rearrange("p i u o -> p i o u")
+            if by_vector:
+                nc.vector.tensor_copy(out=out, in_=in_words)
+            else:
+                nc.scalar.copy(out=out, in_=in_words)
 
-        def w_quantise(s):
-            for j in tiles_of(s):
-                w_codes[j] = work.tile([P, PASSES * P], U32, name="w_codes", align_bytes=64)
-                w_scales[j] = work.tile([P, PASSES * P], U8, name="w_scales", align_bytes=64)
-                nc.vector.quantize_mx(
-                    out=w_codes[j][:].bitcast(FP8X4), scales=w_scales[j][:], in_=w_grouped[j][:]
+        def w_quantise(j):
+            w_codes[j] = work.tile([P, PASSES * P], U32, name="w_codes", align_bytes=64)
+            w_scales[j] = work.tile([P, PASSES * P], U8, name="w_scales", align_bytes=64)
+            nc.vector.quantize_mx(out=w_codes[j][:].bitcast(FP8X4), scales=w_scales[j][:], in_=w_grouped[j][:])
+
+        def multiply(j):
+            product[j] = psum.tile([P, ROWS], F32, name="product", tag="product")
+            for g in range(PASSES):
+                nc.tensor.matmul_mx(
+                    out=product[j][:],
+                    lhsT=w_codes[j][:, g * P : (g + 1) * P].bitcast(FP8X4),
+                    lhsT_scale=w_scales[j][:, g * P : (g + 1) * P],
+                    rhs=vi_codes[:, g, :].bitcast(FP8X4),
+                    rhs_scale=vi_scales[:, g, :],
+                    start=(g == 0),
+                    stop=(g == PASSES - 1),
                 )
 
-        def multiply(s):
-            for j in tiles_of(s):
-                product[j] = psum.tile([P, ROWS], F32, name="product", tag="product")
-                for g in range(PASSES):
-                    nc.tensor.matmul_mx(
-                        out=product[j][:],
-                        lhsT=w_codes[j][:, g * P : (g + 1) * P].bitcast(FP8X4),
-                        lhsT_scale=w_scales[j][:, g * P : (g + 1) * P],
-                        rhs=vi_codes[:, g, :].bitcast(FP8X4),
-                        rhs_scale=vi_scales[:, g, :],
-                        start=(g == 0),
-                        stop=(g == PASSES - 1),
-                    )
+        def bias_relu_and_sum(j):
+            vj[j] = work.tile([P, ROWS], F32, name="vj", bufs=3 * STEP)
+            nc.scalar.activation(
+                out=vj[j][:],
+                in_=product[j][:],
+                func=ACT.Relu,
+                bias=b_col[:, j : j + 1],
+                scale=1.0,
+                accum_out=colsum[:, j : j + 1],
+            )
 
-        def bias_relu_and_sum(s):
-            for j in tiles_of(s):
-                vj[j] = work.tile([P, ROWS], F32, name="vj", bufs=(BACK_LAG + 1) * STEP)
-                nc.scalar.activation(
-                    out=vj[j][:],
-                    in_=product[j][:],
-                    func=ACT.Relu,
-                    bias=b_col[:, j : j + 1],
-                    scale=1.0,
-                    accum_out=colsum[:, j : j + 1],
-                )
+        def spread_column_sums(s):
+            mean_bank[s] = psum.tile([P, STEP, P], F32, name="mean_bank", tag="transposed", bufs=TRANSPOSE_BANKS)
+            for a in range(STEP):
+                j = s * STEP + a
+                nc.tensor.transpose(mean_bank[s][:, a, :], colsum[:, j : j + 1].to_broadcast([P, P]), ident[:])
 
-        def correct(s):
-            for j in tiles_of(s):
-                nc.vector.scalar_tensor_tensor(
-                    out=vj[j][:],
-                    in0=rowsum_scaled[:],
-                    scalar=colsum[:, j : j + 1],
-                    in1=vj[j][:],
-                    op0=ALU.mult,
-                    op1=ALU.add,
-                )
+        def scale_to_mean(s):
+            nc.scalar.mul(
+                out=mean[:, s * STEP_OUTS : (s + 1) * STEP_OUTS],
+                in_=mean_bank[s][:].rearrange("p a o -> p (a o)"),
+                mul=1.0 / ROWS,
+            )
 
         def transpose_back(s):
-            for j in tiles_of(s):
-                back[j] = psum.tile([P, ROW_TILES, P], F32, name="back", tag="transposed", bufs=TRANSPOSE_BANKS)
-                for rt in range(ROW_TILES):
-                    nc.tensor.transpose(back[j][:, rt, :], vj[j][:, rt * P : (rt + 1) * P], ident[:])
+            for h in range(ROW_TILES // RT_PER_BANK):
+                back[s, h] = psum.tile([P, RT_PER_BANK, STEP_OUTS], F32, name="back_bank", tag="transposed", bufs=TRANSPOSE_BANKS)
+                for a in range(STEP):
+                    for i in range(RT_PER_BANK):
+                        rt = h * RT_PER_BANK + i
+                        nc.tensor.transpose(
+                            back[s, h][:, i, a * P : (a + 1) * P],
+                            vj[s * STEP + a][:, rt * P : (rt + 1) * P],
+                            ident[:],
+                        )
 
-        def copy_out_and_store(s):
-            for j in tiles_of(s):
-                result = work.tile([P, ROW_TILES, P], F32, name="result")
-                empty_bank(nc, by_vector=(j == (s + 1) * STEP - 1), out=result[:], in_=back[j][:])
+        def correct_and_store(s):
+            outs = slice(s * STEP_OUTS, (s + 1) * STEP_OUTS)
+            for h in range(ROW_TILES // RT_PER_BANK):
+                result = work.tile([P, RT_PER_BANK, STEP_OUTS], F32, name="result")
+                for i in range(RT_PER_BANK):
+                    rt = h * RT_PER_BANK + i
+                    nc.vector.scalar_tensor_tensor(
+                        out=result[:, i, :],
+                        in0=mean[:, outs],
+                        scalar=rowsum_c[:, rt : rt + 1],
+                        in1=back[s, h][:, i, :],
+                        op0=ALU.mult,
+                        op1=ALU.add,
+                    )
+                rows = slice(h * RT_PER_BANK * P, (h + 1) * RT_PER_BANK * P)
                 nc.sync.dma_start(
-                    out=out_0[:, j * P : (j + 1) * P].rearrange("(t p) o -> p t o", p=P), in_=result[:]
+                    out=out_0[rows, outs].rearrange("(i p) o -> p i o", p=P), in_=result[:]
                 )
 
-        def store_mean():
-            sums_as_rows = psum.tile([P, P], F32, tag="transposed", bufs=TRANSPOSE_BANKS)
-            nc.tensor.transpose(sums_as_rows[:], colsum[:], ident[:])
-            mean_rows = keep.tile([OUT_TILES, P], F32)
-            nc.scalar.mul(out=mean_rows[:], in_=sums_as_rows[0:OUT_TILES, :], mul=1.0 / ROWS)
-            nc.sync.dma_start(out=out_1.rearrange("(j p) -> j p", p=P), in_=mean_rows[:])
+        def keep_clock(n):
+            for i in range(n):
+                bank = psum.tile([P, ROWS], F32, name="clock_bank", tag="product")
+                nc.tensor.matmul(out=bank[:], lhsT=ones[:, 0:P], rhs=ones[:], start=True, stop=True)
 
-        for rt in range(ROW_TILES):
-            vi_transpose_and_regroup(rt)
-            if rt == 0:
-                b_as_columns = psum.tile([P, P], F32, tag="transposed", bufs=TRANSPOSE_BANKS)
-                nc.tensor.transpose(b_as_columns[:], b_square[:], ident[:])
-                nc.vector.tensor_copy(out=b_col[:], in_=b_as_columns[:, 0:OUT_TILES])
-            else:
-                vi_sum_rows(rt - 1)
-            vi_quantise(rt)
-        w_split_words(0)
+        def vi_half(rt, half):
+            vi_transpose(rt, half)
+            vi_regroup(rt, half)
+
+        keep_clock(WARM_UPS)
+        nc.vector.tensor_copy(out=b_square[0:OUT_TILES, :], in_=b_rows[:])
+        vi_half(0, 0)
+        b_as_columns = psum.tile([P, P], F32, tag="product")
+        nc.tensor.transpose(b_as_columns[:], b_square[:], ident[:])
+        vi_half(0, 1)
+        keep_clock(1)
+        vi_sum_rows(0)
+        nc.vector.tensor_copy(out=b_col[:], in_=b_as_columns[:, 0:OUT_TILES])
+        vi_quantise(0, 0)
+        vi_quantise(0, 1)
+        vi_half(1, 0)
+        keep_clock(1)
+        vi_half(1, 1)
+        vi_sum_rows(1)
+        vi_quantise(1, 0)
+        vi_quantise(1, 1)
+        vi_half(2, 0)
+        keep_clock(1)
+        vi_half(2, 1)
+        vi_quantise(2, 0)
+        vi_quantise(2, 1)
         w_transpose(0)
-        w_regroup(0)
-        w_split_words(1)
-        vi_sum_rows(ROW_TILES - 1)
-        nc.vector.tensor_scalar_mul(out=rowsum_scaled[:], in0=rowsum_raw[:], scalar1=C / ROWS)
+        keep_clock(1)
+        w_regroup(0, 0)
+        w_regroup(0, 1, by_vector=True)
         w_quantise(0)
+        vi_half(3, 0)
+        vi_half(3, 1)
+        w_transpose(1)
+        vi_quantise(3, 0)
+        vi_quantise(3, 1)
+        w_regroup(1, 0)
+        w_regroup(1, 1, by_vector=True)
+        multiply(0)
+        w_quantise(1)
+        bias_relu_and_sum(0)
+        vi_sum_rows(2)
+        w_transpose(2)
+        w_regroup(2, 0)
+        w_regroup(2, 1)
+        w_quantise(2)
+        multiply(1)
+        w_split_words(4)
+        w_split_words(5)
+        bias_relu_and_sum(1)
+        w_transpose(3)
+        w_regroup(3, 0)
+        w_regroup(3, 1)
+        w_quantise(3)
+        vi_sum_rows(3)
+        nc.vector.tensor_scalar_mul(out=rowsum_c[:], in0=rowsum[:], scalar1=C)
 
-        for i in range(STEPS + BACK_LAG):
-            if i + 2 < STEPS:
-                w_split_words(i + 2)
-            if i + 1 < STEPS:
-                w_transpose(i + 1)
-                w_regroup(i + 1)
-            if 1 <= i <= STEPS:
-                correct(i - 1)
-            if i >= BACK_LAG:
-                transpose_back(i - BACK_LAG)
-                copy_out_and_store(i - BACK_LAG)
-            if i == STEPS:
-                store_mean()
-            if i + 1 < STEPS:
-                w_quantise(i + 1)
-            if i < STEPS:
-                multiply(i)
-                bias_relu_and_sum(i)
+        for s in range(1, STEPS + 1):
+            first_next = (s + 1) * STEP
+            returned = {STEPS - 1: range(s - 2, s), STEPS: range(s - 1, s)}
+            returning = returned.get(s, range(max(s - 2, 0), s - 1))
+            if s + 1 < STEPS:
+                w_transpose(first_next)
+                w_transpose(first_next + 1)
+                w_regroup(first_next, 0)
+                w_regroup(first_next, 1)
+            for q in returning:
+                spread_column_sums(q)
+                transpose_back(q)
+                scale_to_mean(q)
+            if s + 2 < STEPS:
+                w_split_words(first_next + 2)
+            if s + 1 < STEPS:
+                w_quantise(first_next)
+                w_regroup(first_next + 1, 0)
+                w_regroup(first_next + 1, 1)
+            for q in returning:
+                correct_and_store(q)
+            if s + 2 < STEPS:
+                w_split_words(first_next + 3)
+            if s + 1 < STEPS:
+                w_quantise(first_next + 1)
+            if s < STEPS:
+                for j in range(s * STEP, (s + 1) * STEP):
+                    multiply(j)
+                    bias_relu_and_sum(j)
+        nc.sync.dma_start(out=out_1.rearrange("(a o) -> a o", a=1), in_=mean[0:1, :])

@@ -26,10 +26,8 @@ K_HALF = K // HALVES
 WORDS_PER_PASS = K_PASS // 2
 TILE_COLS = PASSES * P * PACK
 
-STEP = 2
-STEPS = OUT_TILES // STEP
-STEP_OUTS = STEP * P
-RT_PER_BANK = 2
+STEPS = [(j, j + 1) for j in range(0, OUT_TILES - 2, 2)] + [(OUT_TILES - 2,), (OUT_TILES - 1,)]
+LAST = len(STEPS) - 1
 TRANSPOSE_BANKS = 6
 WARM_UPS = 4
 
@@ -54,7 +52,7 @@ def tile_optimalnet_pb_kernel(tc, vi, W, b, out_0, out_1):
     nc = tc.nc
     with ExitStack() as stack:
         keep = stack.enter_context(tc.tile_pool(name="keep", bufs=1))
-        work = stack.enter_context(tc.tile_pool(name="work", bufs=2 * STEP))
+        work = stack.enter_context(tc.tile_pool(name="work", bufs=4))
         psum = stack.enter_context(tc.psum_pool(name="psum", bufs=2))
         stack.enter_context(tc.manual_schedule())
 
@@ -148,6 +146,13 @@ def tile_optimalnet_pb_kernel(tc, vi, W, b, out_0, out_1):
         mean_bank = {}
         back = {}
 
+        def outs_of(s):
+            return slice(STEPS[s][0] * P, (STEPS[s][-1] + 1) * P)
+
+        def row_tiles_of(s, h):
+            count = ROW_TILES // len(STEPS[s])
+            return range(h * count, (h + 1) * count)
+
         def w_split_words(j):
             w_split[j] = work.tile([P, PASSES, 2, P], F32, name="w_split")
             nc.vector.tensor_copy(
@@ -195,7 +200,7 @@ def tile_optimalnet_pb_kernel(tc, vi, W, b, out_0, out_1):
                 )
 
         def bias_relu_and_sum(j):
-            vj[j] = work.tile([P, ROWS], F32, name="vj", bufs=3 * STEP)
+            vj[j] = work.tile([P, ROWS], F32, name="vj", bufs=6)
             nc.scalar.activation(
                 out=vj[j][:],
                 in_=product[j][:],
@@ -206,36 +211,35 @@ def tile_optimalnet_pb_kernel(tc, vi, W, b, out_0, out_1):
             )
 
         def spread_column_sums(s):
-            mean_bank[s] = psum.tile([P, STEP, P], F32, name="mean_bank", tag="transposed", bufs=TRANSPOSE_BANKS)
-            for a in range(STEP):
-                j = s * STEP + a
+            mean_bank[s] = psum.tile([P, len(STEPS[s]), P], F32, name="mean_bank", tag="transposed", bufs=TRANSPOSE_BANKS)
+            for a, j in enumerate(STEPS[s]):
                 nc.tensor.transpose(mean_bank[s][:, a, :], colsum[:, j : j + 1].to_broadcast([P, P]), ident[:])
 
         def scale_to_mean(s):
             nc.scalar.mul(
-                out=mean[:, s * STEP_OUTS : (s + 1) * STEP_OUTS],
+                out=mean[:, outs_of(s)],
                 in_=mean_bank[s][:].rearrange("p a o -> p (a o)"),
                 mul=1.0 / ROWS,
             )
 
         def transpose_back(s):
-            for h in range(ROW_TILES // RT_PER_BANK):
-                back[s, h] = psum.tile([P, RT_PER_BANK, STEP_OUTS], F32, name="back_bank", tag="transposed", bufs=TRANSPOSE_BANKS)
-                for a in range(STEP):
-                    for i in range(RT_PER_BANK):
-                        rt = h * RT_PER_BANK + i
+            tiles = STEPS[s]
+            for h in range(len(tiles)):
+                back[s, h] = psum.tile(
+                    [P, ROW_TILES // len(tiles), len(tiles) * P], F32, name="back_bank", tag="transposed", bufs=TRANSPOSE_BANKS
+                )
+                for a, j in enumerate(tiles):
+                    for i, rt in enumerate(row_tiles_of(s, h)):
                         nc.tensor.transpose(
-                            back[s, h][:, i, a * P : (a + 1) * P],
-                            vj[s * STEP + a][:, rt * P : (rt + 1) * P],
-                            ident[:],
+                            back[s, h][:, i, a * P : (a + 1) * P], vj[j][:, rt * P : (rt + 1) * P], ident[:]
                         )
 
         def correct_and_store(s):
-            outs = slice(s * STEP_OUTS, (s + 1) * STEP_OUTS)
-            for h in range(ROW_TILES // RT_PER_BANK):
-                result = work.tile([P, RT_PER_BANK, STEP_OUTS], F32, name="result")
-                for i in range(RT_PER_BANK):
-                    rt = h * RT_PER_BANK + i
+            outs = outs_of(s)
+            for h in range(len(STEPS[s])):
+                row_tiles = row_tiles_of(s, h)
+                result = work.tile([P, len(row_tiles), outs.stop - outs.start], F32, name="result", bufs=8)
+                for i, rt in enumerate(row_tiles):
                     nc.vector.scalar_tensor_tensor(
                         out=result[:, i, :],
                         in0=mean[:, outs],
@@ -244,44 +248,35 @@ def tile_optimalnet_pb_kernel(tc, vi, W, b, out_0, out_1):
                         op0=ALU.mult,
                         op1=ALU.add,
                     )
-                rows = slice(h * RT_PER_BANK * P, (h + 1) * RT_PER_BANK * P)
-                nc.sync.dma_start(
-                    out=out_0[rows, outs].rearrange("(i p) o -> p i o", p=P), in_=result[:]
-                )
-
-        def keep_clock(n):
-            for i in range(n):
-                bank = psum.tile([P, ROWS], F32, name="clock_bank", tag="product")
-                nc.tensor.matmul(out=bank[:], lhsT=ones[:, 0:P], rhs=ones[:], start=True, stop=True)
+                rows = slice(row_tiles.start * P, row_tiles.stop * P)
+                nc.sync.dma_start(out=out_0[rows, outs].rearrange("(i p) o -> p i o", p=P), in_=result[:])
 
         def vi_half(rt, half):
             vi_transpose(rt, half)
             vi_regroup(rt, half)
 
-        keep_clock(WARM_UPS)
+        for i in range(WARM_UPS):
+            warm_bank = psum.tile([P, ROWS], F32, name="warm_bank", tag="product")
+            nc.tensor.matmul(out=warm_bank[:], lhsT=ones[:, 0:P], rhs=ones[:], start=True, stop=True)
         nc.vector.tensor_copy(out=b_square[0:OUT_TILES, :], in_=b_rows[:])
         vi_half(0, 0)
         b_as_columns = psum.tile([P, P], F32, tag="product")
         nc.tensor.transpose(b_as_columns[:], b_square[:], ident[:])
         vi_half(0, 1)
-        keep_clock(1)
         vi_sum_rows(0)
         nc.vector.tensor_copy(out=b_col[:], in_=b_as_columns[:, 0:OUT_TILES])
         vi_quantise(0, 0)
         vi_quantise(0, 1)
         vi_half(1, 0)
-        keep_clock(1)
         vi_half(1, 1)
         vi_sum_rows(1)
         vi_quantise(1, 0)
         vi_quantise(1, 1)
         vi_half(2, 0)
-        keep_clock(1)
         vi_half(2, 1)
         vi_quantise(2, 0)
         vi_quantise(2, 1)
         w_transpose(0)
-        keep_clock(1)
         w_regroup(0, 0)
         w_regroup(0, 1, by_vector=True)
         w_quantise(0)
@@ -311,33 +306,32 @@ def tile_optimalnet_pb_kernel(tc, vi, W, b, out_0, out_1):
         vi_sum_rows(3)
         nc.vector.tensor_scalar_mul(out=rowsum_c[:], in0=rowsum[:], scalar1=C)
 
-        for s in range(1, STEPS + 1):
-            first_next = (s + 1) * STEP
-            returned = {STEPS - 1: range(s - 2, s), STEPS: range(s - 1, s)}
-            returning = returned.get(s, range(max(s - 2, 0), s - 1))
-            if s + 1 < STEPS:
-                w_transpose(first_next)
-                w_transpose(first_next + 1)
-                w_regroup(first_next, 0)
-                w_regroup(first_next, 1)
+        for s in range(1, LAST + 2):
+            next_tiles = STEPS[s + 1] if s < LAST else ()
+            later_tiles = STEPS[s + 2] if s + 1 < LAST else ()
+            returning = range(max(s - 2, 0), s - 1) if s <= LAST else range(LAST - 1, LAST + 1)
+            for j in next_tiles:
+                w_transpose(j)
+            for half in range(HALVES if next_tiles else 0):
+                w_regroup(next_tiles[0], half)
             for q in returning:
                 spread_column_sums(q)
                 transpose_back(q)
                 scale_to_mean(q)
-            if s + 2 < STEPS:
-                w_split_words(first_next + 2)
-            if s + 1 < STEPS:
-                w_quantise(first_next)
-                w_regroup(first_next + 1, 0)
-                w_regroup(first_next + 1, 1)
+            for j in later_tiles[:1]:
+                w_split_words(j)
+            for j in next_tiles[:1]:
+                w_quantise(j)
+            for j in next_tiles[1:]:
+                for half in range(HALVES):
+                    w_regroup(j, half)
             for q in returning:
                 correct_and_store(q)
-            if s + 2 < STEPS:
-                w_split_words(first_next + 3)
-            if s + 1 < STEPS:
-                w_quantise(first_next + 1)
-            if s < STEPS:
-                for j in range(s * STEP, (s + 1) * STEP):
-                    multiply(j)
-                    bias_relu_and_sum(j)
+            for j in later_tiles[1:]:
+                w_split_words(j)
+            for j in next_tiles[1:]:
+                w_quantise(j)
+            for j in STEPS[s] if s <= LAST else ():
+                multiply(j)
+                bias_relu_and_sum(j)
         nc.sync.dma_start(out=out_1.rearrange("(a o) -> a o", a=1), in_=mean[0:1, :])

@@ -200,7 +200,7 @@ def tile_optimalnet_pb_kernel(tc, vi, W, b, out_0, out_1):
                 )
 
         def bias_relu_and_sum(j):
-            vj[j] = work.tile([P, ROWS], F32, name="vj", bufs=6)
+            vj[j] = work.tile([P, ROWS], F32, name="vj", bufs=8)
             nc.scalar.activation(
                 out=vj[j][:],
                 in_=product[j][:],
@@ -285,31 +285,32 @@ def tile_optimalnet_pb_kernel(tc, vi, W, b, out_0, out_1):
         w_transpose(1)
         vi_quantise(3, 0)
         vi_quantise(3, 1)
+        w_split_words(2)
         w_regroup(1, 0)
-        w_regroup(1, 1, by_vector=True)
+        w_regroup(1, 1)
         multiply(0)
         w_quantise(1)
         bias_relu_and_sum(0)
-        vi_sum_rows(2)
+        w_split_words(3)
         w_transpose(2)
+        w_split_words(4)
         w_regroup(2, 0)
         w_regroup(2, 1)
         w_quantise(2)
         multiply(1)
-        w_split_words(4)
         w_split_words(5)
+        vi_sum_rows(2)
         bias_relu_and_sum(1)
         w_transpose(3)
         w_regroup(3, 0)
         w_regroup(3, 1)
         w_quantise(3)
-        vi_sum_rows(3)
-        nc.vector.tensor_scalar_mul(out=rowsum_c[:], in0=rowsum[:], scalar1=C)
 
+        returns = {3: (0,), 4: (1,), 5: (2,), 6: (3, 4), 7: (5,), 8: (6,), 9: (7, 8)}
         for s in range(1, LAST + 2):
             next_tiles = STEPS[s + 1] if s < LAST else ()
             later_tiles = STEPS[s + 2] if s + 1 < LAST else ()
-            returning = range(max(s - 2, 0), s - 1) if s <= LAST else range(LAST - 1, LAST + 1)
+            returning = returns.get(s, ())
             for j in next_tiles:
                 w_transpose(j)
             for half in range(HALVES if next_tiles else 0):
@@ -331,6 +332,9 @@ def tile_optimalnet_pb_kernel(tc, vi, W, b, out_0, out_1):
                 w_split_words(j)
             for j in next_tiles[1:]:
                 w_quantise(j)
+            if s == 2:
+                vi_sum_rows(3)
+                nc.vector.tensor_scalar_mul(out=rowsum_c[:], in0=rowsum[:], scalar1=C)
             for j in STEPS[s] if s <= LAST else ():
                 multiply(j)
                 bias_relu_and_sum(j)

@@ -28,6 +28,7 @@ TILE_COLS = PASSES * P * PACK
 
 STEPS = [(j, j + 1) for j in range(0, OUT_TILES - 2, 2)] + [(OUT_TILES - 2,), (OUT_TILES - 1,)]
 LAST = len(STEPS) - 1
+BLOCK = 32
 TRANSPOSE_BANKS = 6
 WARM_UPS = 4
 
@@ -88,8 +89,10 @@ def tile_optimalnet_pb_kernel(tc, vi, W, b, out_0, out_1):
         ident = keep.tile([P, P], F32)
         make_identity(nc, ident[:])
         b_col = keep.tile([P, OUT_TILES], F32)
-        colsum = keep.tile([P, OUT_TILES], F32)
+        colsum = keep.tile([P, P], F32)
+        nc.vector.memset(colsum[:], 0.0)
         mean = keep.tile([P, OUTS], F32)
+        rowsum_spread = keep.tile([P, ROWS], F32)
         rowsum = keep.tile([P, ROW_TILES], F32)
         rowsum_c = keep.tile([P, ROW_TILES], F32)
 
@@ -145,6 +148,40 @@ def tile_optimalnet_pb_kernel(tc, vi, W, b, out_0, out_1):
         vj = {}
         mean_bank = {}
         back = {}
+        turned = {}
+
+        def spread_row_sums():
+            bank = psum.tile([P, ROW_TILES, P], F32, name="rowsum_bank", tag="transposed", bufs=TRANSPOSE_BANKS)
+            for rt in range(ROW_TILES):
+                nc.tensor.transpose(bank[:, rt, :], rowsum_c[:, rt : rt + 1].to_broadcast([P, P]), ident[:])
+            nc.scalar.mul(out=rowsum_spread[:], in_=bank[:].rearrange("p t r -> p (t r)"), mul=1.0 / ROWS)
+
+        def correct_turn_and_store(j):
+            nc.vector.scalar_tensor_tensor(
+                out=vj[j][:],
+                in0=rowsum_spread[:],
+                scalar=colsum[:, j : j + 1],
+                in1=vj[j][:],
+                op0=ALU.mult,
+                op1=ALU.add,
+            )
+            turned[j] = work.tile([P, ROWS], F32, name="turned", align_bytes=64)
+
+        def turn_and_store(j):
+            nc.vector.transpose(out=turned[j][:], in_=vj[j][:])
+            for i in range(P // BLOCK):
+                outs = slice(j * P + i * BLOCK, j * P + (i + 1) * BLOCK)
+                nc.sync.dma_start(
+                    out=out_0[:, outs].rearrange("(b r) o -> r b o", r=BLOCK),
+                    in_=turned[j][i * BLOCK : (i + 1) * BLOCK, :].rearrange("r (b o) -> r b o", o=BLOCK),
+                )
+
+        def store_mean():
+            bank = psum.tile([P, P], F32, name="mean_rows_bank", tag="transposed", bufs=TRANSPOSE_BANKS)
+            nc.tensor.transpose(bank[:], colsum[:], ident[:])
+            mean_rows = keep.tile([OUT_TILES, P], F32)
+            nc.scalar.mul(out=mean_rows[:], in_=bank[0:OUT_TILES, :], mul=1.0 / ROWS)
+            nc.scalar.dma_start(out=out_1.rearrange("(j p) -> j p", p=P), in_=mean_rows[:])
 
         def outs_of(s):
             return slice(STEPS[s][0] * P, (STEPS[s][-1] + 1) * P)
@@ -200,7 +237,7 @@ def tile_optimalnet_pb_kernel(tc, vi, W, b, out_0, out_1):
                 )
 
         def bias_relu_and_sum(j):
-            vj[j] = work.tile([P, ROWS], F32, name="vj", bufs=8)
+            vj[j] = work.tile([P, ROWS], F32, name="vj", bufs=8, align_bytes=64)
             nc.scalar.activation(
                 out=vj[j][:],
                 in_=product[j][:],
@@ -306,11 +343,13 @@ def tile_optimalnet_pb_kernel(tc, vi, W, b, out_0, out_1):
         w_regroup(3, 1)
         w_quantise(3)
 
-        returns = {3: (0,), 4: (1,), 5: (2,), 6: (3, 4), 7: (5,), 8: (6,), 9: (7, 8)}
+        returns = {3: (0,), 4: (1,), 5: (2,), 7: (5,), 8: (6,), 9: (7, 8)}
+        turns = {5: (6,7), 6: (8,), 7:(9,)}
         for s in range(1, LAST + 2):
             next_tiles = STEPS[s + 1] if s < LAST else ()
             later_tiles = STEPS[s + 2] if s + 1 < LAST else ()
             returning = returns.get(s, ())
+            turning = turns.get(s, ())
             for j in next_tiles:
                 w_transpose(j)
             for half in range(HALVES if next_tiles else 0):
@@ -319,10 +358,16 @@ def tile_optimalnet_pb_kernel(tc, vi, W, b, out_0, out_1):
                 spread_column_sums(q)
                 transpose_back(q)
                 scale_to_mean(q)
+            if s == LAST + 1:
+                store_mean()
             for j in later_tiles[:1]:
                 w_split_words(j)
+            for j in turning:
+                correct_turn_and_store(j)
             for j in next_tiles[:1]:
                 w_quantise(j)
+            for j in turning:
+                turn_and_store(j)
             for j in next_tiles[1:]:
                 for half in range(HALVES):
                     w_regroup(j, half)
@@ -335,7 +380,8 @@ def tile_optimalnet_pb_kernel(tc, vi, W, b, out_0, out_1):
             if s == 2:
                 vi_sum_rows(3)
                 nc.vector.tensor_scalar_mul(out=rowsum_c[:], in0=rowsum[:], scalar1=C)
+            if s == 3:
+                spread_row_sums()
             for j in STEPS[s] if s <= LAST else ():
                 multiply(j)
                 bias_relu_and_sum(j)
-        nc.sync.dma_start(out=out_1.rearrange("(a o) -> a o", a=1), in_=mean[0:1, :])

@@ -181,7 +181,7 @@ def tile_optimalnet_pb_kernel(tc, vi, W, b, out_0, out_1):
             nc.tensor.transpose(bank[:], colsum[:], ident[:])
             mean_rows = keep.tile([OUT_TILES, P], F32)
             nc.scalar.mul(out=mean_rows[:], in_=bank[0:OUT_TILES, :], mul=1.0 / ROWS)
-            nc.scalar.dma_start(out=out_1.rearrange("(j p) -> j p", p=P), in_=mean_rows[:])
+            nc.sync.dma_start(out=out_1.rearrange("(j p) -> j p", p=P), in_=mean_rows[:])
 
         def outs_of(s):
             return slice(STEPS[s][0] * P, (STEPS[s][-1] + 1) * P)
@@ -295,18 +295,18 @@ def tile_optimalnet_pb_kernel(tc, vi, W, b, out_0, out_1):
         for i in range(WARM_UPS):
             warm_bank = psum.tile([P, ROWS], F32, name="warm_bank", tag="product")
             nc.tensor.matmul(out=warm_bank[:], lhsT=ones[:, 0:P], rhs=ones[:], start=True, stop=True)
-        nc.vector.tensor_copy(out=b_square[0:OUT_TILES, :], in_=b_rows[:])
         vi_half(0, 0)
-        b_as_columns = psum.tile([P, P], F32, tag="product")
-        nc.tensor.transpose(b_as_columns[:], b_square[:], ident[:])
         vi_half(0, 1)
         vi_sum_rows(0)
-        nc.vector.tensor_copy(out=b_col[:], in_=b_as_columns[:, 0:OUT_TILES])
+        nc.vector.tensor_copy(out=b_square[0:OUT_TILES, :], in_=b_rows[:])
         vi_quantise(0, 0)
         vi_quantise(0, 1)
         vi_half(1, 0)
         vi_half(1, 1)
         vi_sum_rows(1)
+        b_as_columns = psum.tile([P, P], F32, tag="product")
+        nc.tensor.transpose(b_as_columns[:], b_square[:], ident[:])
+        nc.vector.tensor_copy(out=b_col[:], in_=b_as_columns[:, 0:OUT_TILES])
         vi_quantise(1, 0)
         vi_quantise(1, 1)
         vi_half(2, 0)
@@ -343,13 +343,12 @@ def tile_optimalnet_pb_kernel(tc, vi, W, b, out_0, out_1):
         w_regroup(3, 1)
         w_quantise(3)
 
-        returns = {3: (0,), 4: (1,), 5: (2,), 7: (5,), 8: (6,), 9: (7, 8)}
-        turns = {5: (6,7), 6: (8,), 7:(9,)}
+        returns = {3: (2,), 5: (3,), 6: (4,), 7: (5, 6), 9: (7, 8)}
+        vector_returns = {4: ((correct_turn_and_store, 0), (correct_turn_and_store, 1), (correct_turn_and_store, 2),), 5: ((turn_and_store, 0), (turn_and_store, 1), (correct_turn_and_store, 3),), 6: ((turn_and_store, 2), (turn_and_store, 3),)}
         for s in range(1, LAST + 2):
             next_tiles = STEPS[s + 1] if s < LAST else ()
             later_tiles = STEPS[s + 2] if s + 1 < LAST else ()
             returning = returns.get(s, ())
-            turning = turns.get(s, ())
             for j in next_tiles:
                 w_transpose(j)
             for half in range(HALVES if next_tiles else 0):
@@ -358,16 +357,12 @@ def tile_optimalnet_pb_kernel(tc, vi, W, b, out_0, out_1):
                 spread_column_sums(q)
                 transpose_back(q)
                 scale_to_mean(q)
-            if s == LAST + 1:
-                store_mean()
             for j in later_tiles[:1]:
                 w_split_words(j)
-            for j in turning:
-                correct_turn_and_store(j)
+            for work_item, j in vector_returns.get(s, ()):
+                work_item(j)
             for j in next_tiles[:1]:
                 w_quantise(j)
-            for j in turning:
-                turn_and_store(j)
             for j in next_tiles[1:]:
                 for half in range(HALVES):
                     w_regroup(j, half)
@@ -385,3 +380,4 @@ def tile_optimalnet_pb_kernel(tc, vi, W, b, out_0, out_1):
             for j in STEPS[s] if s <= LAST else ():
                 multiply(j)
                 bias_relu_and_sum(j)
+        store_mean()

from contextlib import ExitStack

import concourse.mybir as mybir
from concourse.masks import make_identity

F32 = mybir.dt.float32
BF16 = mybir.dt.bfloat16
U32 = mybir.dt.uint32
U8 = mybir.dt.uint8
FP8X4 = mybir.dt.float8_e4m3fn_x4
ALU = mybir.AluOpType
ACT = mybir.ActivationFunctionType

P = 128
PACK = 4
K_PASS = P * PACK
ROWS = 512
K = 2048
OUTS = 2048
PASSES = K // K_PASS
ROW_TILES = ROWS // P
OUT_TILES = OUTS // P
HALVES = 2
PASSES_PER_BANK = PASSES // HALVES
K_HALF = K // HALVES
WORDS_PER_PASS = K_PASS // 2
TILE_COLS = PASSES * P * PACK

STEPS = [(j, j + 1) for j in range(0, OUT_TILES - 2, 2)] + [(OUT_TILES - 2,), (OUT_TILES - 1,)]
LAST = len(STEPS) - 1
BLOCK = 32
TRANSPOSE_BANKS = 6
WARM_UPS = 4

C = 0.01 * 0.001 / 1
FLOPS = 2 * ROWS * K * OUTS


def transpose_every_second_word(nc, bank, words, ident):
    for i in range(PASSES_PER_BANK):
        for u in range(2):
            every_second = slice(i * WORDS_PER_PASS + u, (i + 1) * WORDS_PER_PASS, 2)
            nc.tensor.transpose(bank[:, i, u, :], words[:, every_second], ident[:])


def transpose_split_words(nc, bank, words, ident):
    for i in range(PASSES_PER_BANK):
        for u in range(2):
            nc.tensor.transpose(bank[:, i, u, :], words[:, i, u, :], ident[:])


def tile_optimalnet_pb_kernel(tc, vi, W, b, out_0, out_1):
    nc = tc.nc
    with ExitStack() as stack:
        keep = stack.enter_context(tc.tile_pool(name="keep", bufs=1))
        work = stack.enter_context(tc.tile_pool(name="work", bufs=4))
        psum = stack.enter_context(tc.psum_pool(name="psum", bufs=2))
        stack.enter_context(tc.manual_schedule())

        b_rows = keep.tile([OUT_TILES, P], BF16)
        nc.scalar.dma_start(out=b_rows[:], in_=b.rearrange("(j p) -> j p", p=P))
        vi_rows = {}
        w_rows = {}

        def load_vi(rt):
            for half in range(HALVES):
                rows = keep.tile([P, K_HALF], BF16, name="vi_rows%d_%d" % (rt, half))
                nc.sync.dma_start(
                    out=rows[:], in_=vi[rt * P : (rt + 1) * P, half * K_HALF : (half + 1) * K_HALF]
                )
                vi_rows[rt, half] = rows

        def load_w(j):
            rows = keep.tile([P, K], BF16, name="w_rows%d" % j)
            nc.sync.dma_start(out=rows[:], in_=W[j * P : (j + 1) * P, :])
            w_rows[j] = rows

        for rt in range(ROW_TILES - 1):
            load_vi(rt)
        load_w(0)
        load_vi(ROW_TILES - 1)
        for j in range(1, OUT_TILES):
            load_w(j)

        ones = keep.tile([P, ROWS], BF16)
        nc.vector.memset(ones[:], 1.0)
        b_square = keep.tile([P, P], F32)
        nc.vector.memset(b_square[:], 0.0)
        ident = keep.tile([P, P], F32)
        make_identity(nc, ident[:])
        b_col = keep.tile([P, OUT_TILES], F32)
        colsum = keep.tile([P, P], F32)
        nc.vector.memset(colsum[:], 0.0)
        mean = keep.tile([P, OUTS], F32)
        rowsum_spread = keep.tile([P, ROWS], F32)
        rowsum = keep.tile([P, ROW_TILES], F32)
        rowsum_c = keep.tile([P, ROW_TILES], F32)

        vi_grouped = keep.tile([P, PASSES * ROWS * PACK], BF16, align_bytes=64)
        vi_grouped_words = vi_grouped[:].bitcast(F32).rearrange("p (g r u) -> p g r u", g=PASSES, u=2)
        vi_grouped_cols = vi_grouped[:].rearrange("p (g c) -> p g c", g=PASSES)
        vi_codes = keep.tile([P, PASSES, ROWS], U32, align_bytes=64)
        vi_scales = keep.tile([P, PASSES, ROWS], U8, align_bytes=64)

        def forward_bank():
            return psum.tile([P, PASSES_PER_BANK, 2, P], F32, name="bank", tag="transposed", bufs=TRANSPOSE_BANKS)

        vi_banks = {}

        def vi_transpose(rt, half):
            vi_banks[rt, half] = forward_bank()
            transpose_every_second_word(nc, vi_banks[rt, half], vi_rows[rt, half][:].bitcast(F32), ident)

        def vi_regroup(rt, half):
            nc.scalar.copy(
                out=vi_grouped_words[
                    :, half * PASSES_PER_BANK : (half + 1) * PASSES_PER_BANK, rt * P : (rt + 1) * P, :
                ],
                in_=vi_banks[rt, half][:].rearrange("p i u r -> p i r u"),
            )

        def vi_quantise(rt, half):
            for g in range(half * PASSES_PER_BANK, (half + 1) * PASSES_PER_BANK):
                nc.vector.quantize_mx(
                    out=vi_codes[:, g, rt * P : (rt + 1) * P].bitcast(FP8X4),
                    scales=vi_scales[:, g, rt * P : (rt + 1) * P],
                    in_=vi_grouped_cols[:, g, rt * P * PACK : (rt + 1) * P * PACK],
                )

        def vi_sum_rows(rt):
            half_sums = work.tile([P, K_HALF], F32, name="half_sums", bufs=1)
            nc.vector.scalar_tensor_tensor(
                out=half_sums[:],
                in0=vi_rows[rt, 0][:],
                scalar=1.0,
                in1=vi_rows[rt, 1][:],
                op0=ALU.mult,
                op1=ALU.add,
                accum_out=rowsum[:, rt : rt + 1],
            )

        w_split = {}
        w_banks = {}
        w_grouped = {}
        w_codes = {}
        w_scales = {}
        product = {}
        vj = {}
        mean_bank = {}
        back = {}
        turned = {}

        def spread_row_sums():
            bank = psum.tile([P, ROW_TILES, P], F32, name="rowsum_bank", tag="transposed", bufs=TRANSPOSE_BANKS)
            for rt in range(ROW_TILES):
                nc.tensor.transpose(bank[:, rt, :], rowsum_c[:, rt : rt + 1].to_broadcast([P, P]), ident[:])
            nc.scalar.mul(out=rowsum_spread[:], in_=bank[:].rearrange("p t r -> p (t r)"), mul=1.0 / ROWS)

        def correct_turn_and_store(j):
            nc.vector.scalar_tensor_tensor(
                out=vj[j][:],
                in0=rowsum_spread[:],
                scalar=colsum[:, j : j + 1],
                in1=vj[j][:],
                op0=ALU.mult,
                op1=ALU.add,
            )
            turned[j] = work.tile([P, ROWS], F32, name="turned", align_bytes=64)

        def turn_and_store(j):
            nc.vector.transpose(out=turned[j][:], in_=vj[j][:])
            for i in range(P // BLOCK):
                outs = slice(j * P + i * BLOCK, j * P + (i + 1) * BLOCK)
                nc.sync.dma_start(
                    out=out_0[:, outs].rearrange("(b r) o -> r b o", r=BLOCK),
                    in_=turned[j][i * BLOCK : (i + 1) * BLOCK, :].rearrange("r (b o) -> r b o", o=BLOCK),
                )

        def store_mean():
            bank = psum.tile([P, P], F32, name="mean_rows_bank", tag="transposed", bufs=TRANSPOSE_BANKS)
            nc.tensor.transpose(bank[:], colsum[:], ident[:])
            mean_rows = keep.tile([OUT_TILES, P], F32)
            nc.scalar.mul(out=mean_rows[:], in_=bank[0:OUT_TILES, :], mul=1.0 / ROWS)
            nc.sync.dma_start(out=out_1.rearrange("(j p) -> j p", p=P), in_=mean_rows[:])

        def outs_of(s):
            return slice(STEPS[s][0] * P, (STEPS[s][-1] + 1) * P)

        def row_tiles_of(s, h):
            count = ROW_TILES // len(STEPS[s])
            return range(h * count, (h + 1) * count)

        def w_split_words(j):
            w_split[j] = work.tile([P, PASSES, 2, P], F32, name="w_split")
            nc.vector.tensor_copy(
                out=w_split[j][:],
                in_=w_rows[j][:].bitcast(F32).rearrange("p (g w u) -> p g u w", g=PASSES, u=2),
            )

        def w_transpose(j):
            for half in range(HALVES):
                w_banks[j, half] = forward_bank()
                if j in w_split:
                    half_words = w_split[j][:, half * PASSES_PER_BANK : (half + 1) * PASSES_PER_BANK]
                    transpose_split_words(nc, w_banks[j, half], half_words, ident)
                else:
                    half_rows = w_rows[j][:, half * K_HALF : (half + 1) * K_HALF]
                    transpose_every_second_word(nc, w_banks[j, half], half_rows.bitcast(F32), ident)

        def w_regroup(j, half, by_vector=False):
            if half == 0:
                w_grouped[j] = work.tile([P, TILE_COLS], BF16, name="w_grouped", align_bytes=64)
            grouped_words = w_grouped[j][:].bitcast(F32).rearrange("p (g o u) -> p g o u", g=PASSES, u=2)
            out = grouped_words[:, half * PASSES_PER_BANK : (half + 1) * PASSES_PER_BANK]
            in_words = w_banks[j, half][:].rearrange("p i u o -> p i o u")
            if by_vector:
                nc.vector.tensor_copy(out=out, in_=in_words)
            else:
                nc.scalar.copy(out=out, in_=in_words)

        def w_quantise(j):
            w_codes[j] = work.tile([P, PASSES * P], U32, name="w_codes", align_bytes=64)
            w_scales[j] = work.tile([P, PASSES * P], U8, name="w_scales", align_bytes=64)
            nc.vector.quantize_mx(out=w_codes[j][:].bitcast(FP8X4), scales=w_scales[j][:], in_=w_grouped[j][:])

        def multiply(j):
            product[j] = psum.tile([P, ROWS], F32, name="product", tag="product")
            for g in range(PASSES):
                nc.tensor.matmul_mx(
                    out=product[j][:],
                    lhsT=w_codes[j][:, g * P : (g + 1) * P].bitcast(FP8X4),
                    lhsT_scale=w_scales[j][:, g * P : (g + 1) * P],
                    rhs=vi_codes[:, g, :].bitcast(FP8X4),
                    rhs_scale=vi_scales[:, g, :],
                    start=(g == 0),
                    stop=(g == PASSES - 1),
                )

        def bias_relu_and_sum(j):
            vj[j] = work.tile([P, ROWS], F32, name="vj", bufs=8, align_bytes=64)
            nc.scalar.activation(
                out=vj[j][:],
                in_=product[j][:],
                func=ACT.Relu,
                bias=b_col[:, j : j + 1],
                scale=1.0,
                accum_out=colsum[:, j : j + 1],
            )

        def spread_column_sums(s):
            mean_bank[s] = psum.tile([P, len(STEPS[s]), P], F32, name="mean_bank", tag="transposed", bufs=TRANSPOSE_BANKS)
            for a, j in enumerate(STEPS[s]):
                nc.tensor.transpose(mean_bank[s][:, a, :], colsum[:, j : j + 1].to_broadcast([P, P]), ident[:])

        def scale_to_mean(s):
            nc.scalar.mul(
                out=mean[:, outs_of(s)],
                in_=mean_bank[s][:].rearrange("p a o -> p (a o)"),
                mul=1.0 / ROWS,
            )

        def transpose_back(s):
            tiles = STEPS[s]
            for h in range(len(tiles)):
                back[s, h] = psum.tile(
                    [P, ROW_TILES // len(tiles), len(tiles) * P], F32, name="back_bank", tag="transposed", bufs=TRANSPOSE_BANKS
                )
                for a, j in enumerate(tiles):
                    for i, rt in enumerate(row_tiles_of(s, h)):
                        nc.tensor.transpose(
                            back[s, h][:, i, a * P : (a + 1) * P], vj[j][:, rt * P : (rt + 1) * P], ident[:]
                        )

        def correct_and_store(s):
            outs = outs_of(s)
            for h in range(len(STEPS[s])):
                row_tiles = row_tiles_of(s, h)
                result = work.tile([P, len(row_tiles), outs.stop - outs.start], F32, name="result", bufs=8)
                for i, rt in enumerate(row_tiles):
                    nc.vector.scalar_tensor_tensor(
                        out=result[:, i, :],
                        in0=mean[:, outs],
                        scalar=rowsum_c[:, rt : rt + 1],
                        in1=back[s, h][:, i, :],
                        op0=ALU.mult,
                        op1=ALU.add,
                    )
                rows = slice(row_tiles.start * P, row_tiles.stop * P)
                nc.sync.dma_start(out=out_0[rows, outs].rearrange("(i p) o -> p i o", p=P), in_=result[:])

        def vi_half(rt, half):
            vi_transpose(rt, half)
            vi_regroup(rt, half)

        for i in range(WARM_UPS):
            warm_bank = psum.tile([P, ROWS], F32, name="warm_bank", tag="product")
            nc.tensor.matmul(out=warm_bank[:], lhsT=ones[:, 0:P], rhs=ones[:], start=True, stop=True)
        vi_half(0, 0)
        vi_half(0, 1)
        vi_sum_rows(0)
        nc.vector.tensor_copy(out=b_square[0:OUT_TILES, :], in_=b_rows[:])
        vi_quantise(0, 0)
        vi_quantise(0, 1)
        vi_half(1, 0)
        vi_half(1, 1)
        vi_sum_rows(1)
        b_as_columns = psum.tile([P, P], F32, tag="product")
        nc.tensor.transpose(b_as_columns[:], b_square[:], ident[:])
        nc.vector.tensor_copy(out=b_col[:], in_=b_as_columns[:, 0:OUT_TILES])
        vi_quantise(1, 0)
        vi_quantise(1, 1)
        vi_half(2, 0)
        vi_half(2, 1)
        vi_quantise(2, 0)
        vi_quantise(2, 1)
        w_transpose(0)
        w_regroup(0, 0)
        w_regroup(0, 1, by_vector=True)
        w_quantise(0)
        vi_half(3, 0)
        vi_half(3, 1)
        w_transpose(1)
        vi_quantise(3, 0)
        vi_quantise(3, 1)
        w_split_words(2)
        w_regroup(1, 0)
        w_regroup(1, 1)
        multiply(0)
        w_quantise(1)
        bias_relu_and_sum(0)
        w_split_words(3)
        w_transpose(2)
        w_split_words(4)
        w_regroup(2, 0)
        w_regroup(2, 1)
        w_quantise(2)
        multiply(1)
        w_split_words(5)
        vi_sum_rows(2)
        bias_relu_and_sum(1)
        w_transpose(3)
        w_regroup(3, 0)
        w_regroup(3, 1)
        w_quantise(3)

        returns = {3: (2,), 5: (3,), 6: (4,), 7: (5, 6), 9: (7, 8)}
        vector_returns = {4: ((correct_turn_and_store, 0), (correct_turn_and_store, 1), (correct_turn_and_store, 2),), 5: ((turn_and_store, 0), (turn_and_store, 1), (correct_turn_and_store, 3),), 6: ((turn_and_store, 2), (turn_and_store, 3),)}
        for s in range(1, LAST + 2):
            next_tiles = STEPS[s + 1] if s < LAST else ()
            later_tiles = STEPS[s + 2] if s + 1 < LAST else ()
            returning = returns.get(s, ())
            for j in next_tiles:
                w_transpose(j)
            for half in range(HALVES if next_tiles else 0):
                w_regroup(next_tiles[0], half)
            for q in returning:
                spread_column_sums(q)
                transpose_back(q)
                scale_to_mean(q)
            for j in later_tiles[:1]:
                w_split_words(j)
            for work_item, j in vector_returns.get(s, ()):
                work_item(j)
            for j in next_tiles[:1]:
                w_quantise(j)
            for j in next_tiles[1:]:
                for half in range(HALVES):
                    w_regroup(j, half)
            for q in returning:
                correct_and_store(q)
            for j in later_tiles[1:]:
                w_split_words(j)
            for j in next_tiles[1:]:
                w_quantise(j)
            if s == 2:
                vi_sum_rows(3)
                nc.vector.tensor_scalar_mul(out=rowsum_c[:], in0=rowsum[:], scalar1=C)
            if s == 3:
                spread_row_sums()
            for j in STEPS[s] if s <= LAST else ():
                multiply(j)
                bias_relu_and_sum(j)
        store_mean()
